import numpy as np
import ml_dtypes


def mxq(x, axis, fmt="e4m3"):
    dtype, down = {"e4m3": (ml_dtypes.float8_e4m3fn, 7), "e5m2": (ml_dtypes.float8_e5m2, 14)}[fmt]
    v = np.moveaxis(np.asarray(x, np.float32).astype(ml_dtypes.bfloat16).astype(np.float64), axis, -1)
    blocks = v.reshape(v.shape[:-1] + (-1, 32))
    amax = np.abs(blocks).max(-1, keepdims=True)
    byte = np.maximum(np.where(amax > 0, np.frexp(amax)[1] - 1 + 127, 0) - down, 1)
    scale = np.exp2(byte - 127.0)
    codes = (blocks / scale).astype(np.float32).astype(dtype).astype(np.float64)
    return np.moveaxis((codes * scale).reshape(v.shape), -1, axis)


WIDE = False


def mx_kscale(k):
    if not WIDE:
        return np.ones(k)
    levels = np.array([10, -10, 5, -5, 0])
    if k % 512:
        return np.exp2(np.random.permutation(np.resize(levels, k // 32))).repeat(32)
    a = np.empty((k // 512, 16))
    for p in range(k // 512):
        a[p, :8] = np.random.permutation(np.resize(levels, 8))
        for g in range(8):
            far = levels[np.abs(levels - a[p, g]) >= 10]
            a[p, g + 8] = far[np.random.randint(len(far))]
    return np.exp2(a.ravel()).repeat(32)


BF16 = ml_dtypes.bfloat16


def bf(x):
    return np.asarray(x, np.float32).astype(BF16)


def f64(x):
    return np.asarray(x).astype(np.float64)


H, N, S, T, L, K = 2, 2, 512, 2048, 3072, 512
NH = N * H


def rel_shift(p):
    zero_pad = np.zeros((NH, S, 1))
    padded = np.concatenate([zero_pad, p], axis=2)
    padded = padded.reshape(NH, T + 1, S)
    return padded[:, 1:, :].reshape(NH, S, T)


def rel_unshift(g):
    flat = np.concatenate([np.zeros((NH, S)), g.reshape(NH, S * T)], axis=1)
    return flat.reshape(NH, S, T + 1)[:, :, 1:]


def by_head(a):
    return a.reshape(N, H, S, a.shape[2]).transpose(1, 0, 2, 3).reshape(H, N * S, a.shape[2])


def setup_inputs():
    s = mx_kscale(N * S).reshape(N, 1, S, 1)
    sr = np.broadcast_to(s, (N, H, S, 1)).reshape(NH, S, 1)
    u = mx_kscale(T)
    ur = np.concatenate([u, np.ones(L - T)])[:, None]
    f = rel_shift(u / sr)
    f = np.where(f == 0.0, 1.0, f)
    queries = bf(np.random.standard_normal((NH, S, K)) * sr)
    v_bias = bf(np.random.standard_normal((1, H, 1, K)) / np.sqrt(K) * s.min())
    R = bf(np.random.standard_normal((H, L, K)) / ur)
    g = bf(np.random.standard_normal((NH, S, T)) * np.exp2(np.random.randint(-6, 1, (NH, S, 1))) * 4.0 * f)
    return {"queries": queries, "v_bias": v_bias, "R": R, "grad_out": g}


def reference(queries, v_bias, R, grad_out):
    q = (f64(queries) * K ** -0.5).reshape(N, H, S, K)
    q_v = by_head((q + f64(v_bias)).reshape(NH, S, K))
    r = f64(R)[:, :T, :]
    dpos = by_head(rel_unshift(f64(grad_out)))
    dq_v = mxq(dpos, 2, "e5m2") @ mxq(r, 1, "e4m3")
    dqueries = (dq_v * K ** -0.5).reshape(H, N, S, K).transpose(1, 0, 2, 3).reshape(NH, S, K)
    dr = mxq(dpos, 1, "e5m2").transpose(0, 2, 1) @ mxq(q_v, 1, "e4m3")
    dR = np.concatenate([dr, np.zeros((H, L - T, K))], axis=1)
    return dqueries, dR

@@ -1,0 +1,289 @@
+from contextlib import ExitStack
+
+import concourse.mybir as mybir
+from concourse.masks import make_identity
+
+SEQS, HEADS, S, T, L, K = 2, 2, 512, 2048, 3072, 512
+NB = SEQS * HEADS
+SCALE = K**-0.5
+
+FLOPS = 2 * 2 * NB * S * T * K
+BYTES = 2 * (NB * S * K + HEADS * K + HEADS * T * K + NB * S * T) + 4 * (NB * S * K + HEADS * L * K)
+
+F32 = mybir.dt.float32
+BF16 = mybir.dt.bfloat16
+U32 = mybir.dt.uint32
+U8 = mybir.dt.uint8
+E4M3 = mybir.dt.float8_e4m3fn_x4
+E5M2 = mybir.dt.float8_e5m2_x4
+MULT = mybir.AluOpType.mult
+ADD = mybir.AluOpType.add
+
+P = 128
+ROW = T + 1
+VCOLS = {0: 384}
+
+UNITS = [(1, 0), (1, 1), (3, 0), (3, 1), (1, 2), (1, 3), (3, 2), (3, 3), (2, 0), (2, 1), (2, 2), (2, 3), (0, 0), (0, 1), (0, 2), (0, 3)]
+LOADS0 = [('G', 1, 0, 0), ('V',), ('Q', 1), ('G', 1, 0, 1), ('Q', 3), ('G', 3, 0, 2), ('R', 1, 0), ('G', 1, 1, 2), ('G', 3, 1, 2), ('R', 1, 1), ('G', 2, 0, 2), ('G', 2, 1, 2), ('R', 0, 0), ('R', 0, 1), ('G', 0, 0, 2), ('Q', 2), ('Q', 0), ('G', 0, 1, 2)]
+LATER = {}
+ZEROS = {10: 1, 12: 1, 13: 1, 14: 1}
+TK = {0: [0], 1: [1], 2: [2], 3: [3], 4: [4], 5: [5], 6: [6], 7: [7], 12: [8], 13: [12], 14: [9], 15: [13], 16: [10], 17: [14], 18: [11], 19: [15]}
+QV = {0: 1, 1: 3, 10: 2, 11: 0}
+RR = {3: [(1, 0)], 4: [(1, 1)], 5: [(1, 2)], 6: [(1, 3)], 8: [(0, 0)], 9: [(0, 1)], 10: [(0, 2)], 11: [(0, 3)]}
+O1 = {4: (1, 0), 5: (1, 1), 8: (1, 2), 9: (1, 3), 15: (0, 0), 17: (0, 1), 19: (0, 2), 21: (0, 3)}
+O0 = {7: 1, 10: 3, 13: 2, 16: 0}
+SLOTS = 22
+VSHARE = 20
+
+
+def tile_relativepositionsdpa_pa_v_kernel(tc, queries, v_bias, table, grad_out, dq_out, dr_out):
+    nc = tc.nc
+    flat = grad_out.rearrange("b s t -> (b s t)")
+
+    with ExitStack() as ctx:
+        pool = lambda name, bufs: ctx.enter_context(tc.tile_pool(name=name, bufs=bufs))
+        const = pool("const", 1)
+        gpool = pool("gpool", 6)
+        qpool = pool("qpool", 3)
+        rpool = pool("rpool", 2)
+        stt = pool("stt", 3)
+        stk = pool("stk", 3)
+        strq = pool("strq", 2)
+        trc = pool("trc", 9)
+        tokc = pool("tokc", 6)
+        rcp = pool("rcp", 8)
+        qcp = pool("qcp", 4)
+        opool = pool("opool", 4)
+        ptr = ctx.enter_context(tc.psum_pool(name="ptr", bufs=4))
+        pmm = ctx.enter_context(tc.psum_pool(name="pmm", bufs=4))
+
+        zeros = const.tile([P, K], F32)
+        nc.vector.memset(zeros[:], 0.0)
+        ident = const.tile([P, P], F32)
+        make_identity(nc, ident[:])
+        vrow = const.tile([P, HEADS * K], BF16)
+        nc.vector.memset(vrow[:], 0.0)
+        ones = const.tile([P, P], BF16)
+        nc.vector.memset(ones[:], 1.0)
+        warm = const.tile([P, 1], F32)
+        nc.scalar.mul(warm[:], zeros[:, 0:1], SCALE)
+        vb = const.tile([P, HEADS * K], BF16)
+        first = const.tile([1, 16], BF16)
+
+        grad, qraw, rraw = {}, {}, {}
+        banks, staged = {}, {}
+        codes = {}
+
+        def window(base, rows, part):
+            return flat[base : base + rows * 4 * ROW].rearrange("(p j c) -> p j c", j=4, c=ROW)
+
+        def load_grad(b, half, parts):
+            if (b, half) not in grad:
+                g = gpool.tile([P, 4, 1024], BF16)
+                grad[b, half] = g
+            g = grad[b, half]
+            if b == 0 and half == 0:
+                nc.sync.dma_start(out=g[:, 1:4, 0:512], in_=window(ROW - S, P, 0)[:, 0:3, 1:513])
+                nc.sync.dma_start(out=g[64:128, 0, 0:512], in_=window(64 * 4 * ROW - S, 64, 0)[:, 0, 1:513])
+                nc.sync.dma_start(out=g[1:65, 0, 0:512], in_=window(4 * ROW - S, 64, 0)[:, 0, 1:513])
+                nc.sync.dma_start(out=g[:, :, 512:1024], in_=window(0, P, 0)[:, :, 1:513])
+                nc.sync.dma_start(out=first[:], in_=flat[0:16].rearrange("(a c) -> a c", a=1))
+                return
+            base, c0 = (0, half * 1024 - 512) if b == 0 else (b * S * T - S, half * 1024)
+            for lo, hi in parts:
+                nc.sync.dma_start(out=g[:, :, lo:hi], in_=window(base, P, 0)[:, :, 1 + c0 + lo : 1 + c0 + hi])
+
+        def load(kind, *a):
+            if kind == "G":
+                b, half, part = a
+                load_grad(b, half, [(0, 1024)] if part == 2 else [(part * 512, part * 512 + 512)])
+            elif kind == "Q":
+                q = qpool.tile([P, 4, K], BF16)
+                nc.sync.dma_start(out=q[:], in_=queries[a[0]].rearrange("(p j) k -> p j k", j=4))
+                qraw[a[0]] = q
+            elif kind == "R":
+                h, half = a
+                r = rpool.tile([P, 2, 4, K], BF16)
+                nc.sync.dma_start(
+                    out=r[:],
+                    in_=table[h, half * 1024 : half * 1024 + 1024, :].rearrange("(g p j) k -> p g j k", p=P, j=4),
+                )
+                rraw[h, half] = r
+            elif kind == "V":
+                nc.sync.dma_start(out=vrow[0:1, :], in_=v_bias.rearrange("a h b k -> (a b) (h k)"))
+
+        def store_zeros(i):
+            h, half = divmod(i, 2)
+            rows = slice(T + half * 512, T + half * 512 + 512)
+            nc.sync.dma_start(
+                out=dr_out[h, rows, :].rearrange("(p j) k -> p j k", j=4),
+                in_=zeros[:].unsqueeze(1).to_broadcast([P, 4, K]),
+            )
+
+        def fix_row0(b):
+            g = grad[b, 0]
+            z = zeros[:].bitcast(BF16)
+            if b == 0:
+                nc.scalar.copy(g[0:1, 0, 0:512], z[0:1, 0:512])
+                nc.scalar.copy(g[0:1, 0, 511:512], first[:, 0:1])
+            else:
+                nc.scalar.copy(g[0:1, 0, 0:511], z[0:1, 0:511])
+
+        def quantize(key, cpool, fmt):
+            src = staged.pop(key)
+            code = cpool.tile([P, 512], U32, align_bytes=64)
+            scale = cpool.tile([P, 512], U8, align_bytes=64)
+            nc.vector.quantize_mx(out=code[:].bitcast(fmt), scales=scale[:], in_=src)
+            codes[key] = (code, scale)
+
+        def interleave(dst, src, lo, hi, copy):
+            copy(
+                dst[:, lo:hi, :].rearrange("p (c i) t -> p c t i", i=4),
+                src[:, :, lo:hi].rearrange("p t (c i) -> p c t i", i=4),
+            )
+
+        def both(dst, src, vcols):
+            if vcols:
+                interleave(dst, src, 0, vcols, nc.vector.tensor_copy)
+            if vcols < 512:
+                interleave(dst, src, vcols, 512, nc.scalar.copy)
+
+        def trp(u):
+            b, g = u
+            words = grad[b, g // 2][:].rearrange("p j c -> p (j c)").bitcast(F32)
+            pair = []
+            for jj in range(2):
+                bank = ptr.tile([P, 2, 2, P], F32)
+                for j2 in range(2):
+                    for e in range(2):
+                        w0 = (2 * jj + j2) * 512 + (g % 2) * 256
+                        nc.tensor.transpose(bank[:, j2, e, :], words[:, w0 + e : w0 + 256 : 2], ident[:])
+                pair.append(bank)
+            banks[u] = pair
+
+        def trcopy(u, engs):
+            grouped = stt.tile([P, 4, P, 4], BF16, align_bytes=64)
+            for jj, bank in enumerate(banks.pop(u)):
+                dst = grouped[:, 2 * jj : 2 * jj + 2, :, :].rearrange("p j r t -> p (j r t)").bitcast(F32)
+                dst = dst.rearrange("p (j r e) -> p j r e", j=2, e=2)
+                src = bank[:].rearrange("p j e r -> p j r e")
+                (nc.scalar.copy if engs[jj] == "S" else nc.vector.tensor_copy)(dst, src)
+            staged["T", u] = grouped[:].rearrange("p j r t -> p (j r t)")
+
+        def tki(u, vcols):
+            b, g = u
+            grouped = stk.tile([P, 512, 4], BF16, align_bytes=64)
+            both(grouped, grad[b, g // 2][:, :, (g % 2) * 512 : (g % 2) * 512 + 512], vcols)
+            staged["K", u] = grouped[:].rearrange("p w t -> p (w t)")
+
+        def rri(u, vcols):
+            h, g = u
+            rgrouped = strq.tile([P, 512, 4], BF16, align_bytes=64, tag="rq")
+            both(rgrouped, rraw[h, g // 2][:, g % 2, :, :], vcols)
+            staged["R", u] = rgrouped[:].rearrange("p w t -> p (w t)")
+
+        def qvi(b):
+            h = b % HEADS
+            qgrouped = strq.tile([P, 512, 4], BF16, align_bytes=64, tag="rq")
+            bias = vb[:, h * K : (h + 1) * K].unsqueeze(2).to_broadcast([P, K, 4])
+            nc.vector.scalar_tensor_tensor(
+                out=qgrouped[:],
+                in0=qraw[b][:].rearrange("p t w -> p w t"),
+                scalar=SCALE,
+                in1=bias,
+                op0=MULT,
+                op1=ADD,
+            )
+            staged["Q", b] = qgrouped[:].rearrange("p w t -> p (w t)")
+
+        def product(lhs, rhs, cols, start, stop, acc):
+            (lc, ls), (rc, rs) = codes[lhs], codes[rhs]
+            nc.tensor.matmul_mx(
+                out=acc[:],
+                lhsT=lc[:, cols].bitcast(E5M2),
+                lhsT_scale=ls[:, cols],
+                rhs=rc[:].bitcast(E4M3),
+                rhs_scale=rs[:],
+                start=start,
+                stop=stop,
+            )
+
+        def out1(h, g, engs, pieces):
+            accs = []
+            for m in range(4):
+                acc = pmm.tile([P, 512], F32)
+                for n in range(SEQS):
+                    b = n * HEADS + h
+                    product(("K", (b, g)), ("Q", b), slice(m * P, m * P + P), n == 0, n == SEQS - 1, acc)
+                accs.append(acc)
+            res = opool.tile([P, 4, 512], F32)
+            view = dr_out[h, g * 512 : g * 512 + 512, :].rearrange("(m p) k -> p m k", p=P)
+            step = 4 // pieces
+            for m in range(4):
+                (nc.scalar.copy if engs[m] == "S" else nc.vector.tensor_copy)(res[:, m, :], accs[m][:])
+                if (m + 1) % step == 0:
+                    nc.sync.dma_start(out=view[:, m + 1 - step : m + 1, :], in_=res[:, m + 1 - step : m + 1, :])
+
+        def out0(b, engs):
+            h = b % HEADS
+            accs = []
+            for j in range(4):
+                acc = pmm.tile([P, 512], F32)
+                for g in range(4):
+                    product(("T", (b, g)), ("R", (h, g)), slice(j * P, j * P + P), g == 0, g == 3, acc)
+                accs.append(acc)
+            res = opool.tile([P, 4, 512], F32)
+            for j in range(4):
+                if engs[j] == "S":
+                    nc.scalar.mul(res[:, j, :], accs[j][:], SCALE)
+                else:
+                    nc.vector.tensor_scalar(res[:, j, :], accs[j][:], SCALE, None, op0=MULT)
+            nc.sync.dma_start(out=dq_out[b].rearrange("(p j) k -> p j k", j=4), in_=res[:])
+
+        def quant(kind, u):
+            cpool = {"T": trc, "K": tokc, "R": rcp, "Q": qcp}[kind]
+            quantize((kind, u), cpool, E5M2 if kind in "TK" else E4M3)
+
+        with tc.manual_schedule():
+            for item in LOADS0:
+                load(*item)
+            pend = []
+            zi = 0
+            for s in range(SLOTS):
+                for item in LATER.get(s, []):
+                    load(*item)
+                fresh = []
+                if s < 16:
+                    b, g = UNITS[s]
+                    if g == 0:
+                        fix_row0(b)
+                    trp(UNITS[s])
+                if s == 0:
+                    for h in range(HEADS):
+                        acc = pmm.tile([P, 512], F32)
+                        nc.tensor.matmul(acc[:], lhsT=ones[:], rhs=vrow[:, h * K : (h + 1) * K], start=True, stop=True)
+                        nc.scalar.copy(vb[:, h * K : (h + 1) * K], acc[:])
+                for kind, u in pend:
+                    quant(kind, u)
+                for k in TK.get(s, []):
+                    tki(UNITS[k], VCOLS.get(("K", k), VCOLS[0]))
+                    fresh.append(("K", UNITS[k]))
+                if s < 16:
+                    trcopy(UNITS[s], "SS")
+                if s in QV:
+                    qvi(QV[s])
+                    fresh.append(("Q", QV[s]))
+                for u in RR.get(s, []):
+                    rri(u, VCOLS.get(("R", u), VCOLS[0]))
+                    fresh.append(("R", u))
+                if s < 16:
+                    fresh.append(("T", UNITS[s]))
+                pend = fresh
+                engs = "SSSS" if s < VSHARE else "SVSV"
+                if s in O0:
+                    out0(O0[s], engs)
+                if s in O1:
+                    out1(*O1[s], engs, 4 if s == SLOTS - 1 else 1)
+                for z in range(ZEROS.get(s, 0)):
+                    store_zeros(zi)
+                    zi += 1

@@ -21,19 +21,22 @@ ADD = mybir.AluOpType.add
 
 P = 128
 ROW = T + 1
-VCOLS = {0: 384}
+VCOLS = {'V': 512, 'S': 0, 'H': 256}
 
-UNITS = [(1, 0), (1, 1), (3, 0), (3, 1), (1, 2), (1, 3), (3, 2), (3, 3), (2, 0), (2, 1), (2, 2), (2, 3), (0, 0), (0, 1), (0, 2), (0, 3)]
-LOADS0 = [('G', 1, 0, 0), ('V',), ('Q', 1), ('G', 1, 0, 1), ('Q', 3), ('G', 3, 0, 2), ('R', 1, 0), ('G', 1, 1, 2), ('G', 3, 1, 2), ('R', 1, 1), ('G', 2, 0, 2), ('G', 2, 1, 2), ('R', 0, 0), ('R', 0, 1), ('G', 0, 0, 2), ('Q', 2), ('Q', 0), ('G', 0, 1, 2)]
-LATER = {}
-ZEROS = {10: 1, 12: 1, 13: 1, 14: 1}
-TK = {0: [0], 1: [1], 2: [2], 3: [3], 4: [4], 5: [5], 6: [6], 7: [7], 12: [8], 13: [12], 14: [9], 15: [13], 16: [10], 17: [14], 18: [11], 19: [15]}
-QV = {0: 1, 1: 3, 10: 2, 11: 0}
-RR = {3: [(1, 0)], 4: [(1, 1)], 5: [(1, 2)], 6: [(1, 3)], 8: [(0, 0)], 9: [(0, 1)], 10: [(0, 2)], 11: [(0, 3)]}
-O1 = {4: (1, 0), 5: (1, 1), 8: (1, 2), 9: (1, 3), 15: (0, 0), 17: (0, 1), 19: (0, 2), 21: (0, 3)}
-O0 = {7: 1, 10: 3, 13: 2, 16: 0}
+UNITS = [(1, 0, 0), (1, 0, 1), (1, 1, 0), (1, 1, 1), (3, 0, 0), (3, 0, 1), (3, 1, 0), (3, 1, 1), (2, 0, 0), (2, 0, 1), (2, 1, 0), (2, 1, 1), (0, 0, 0), (0, 0, 1), (0, 1, 0), (0, 1, 1)]
+LOADS0 = [('G', 1, (0,)), ('V',), ('Q', 1), ('G', 1, (1,)), ('G', 1, (2, 3)), ('G', 3, (0, 1)), ('G', 3, (2, 3))]
+LATER = {4: [('Q', 2), ('G', 0, (0,)), ('R', 0, 1), ('Q', 0)], 3: [('R', 0, 0), ('G', 2, (2, 3))], 1: [('G', 2, (0, 1)), ('R', 1, 1)], 0: [('Q', 3), ('R', 1, 0)]}
+ZEROS = {8: 1, 9: 1, 7: 1, 13: 1}
+TK = {2: [(1, 1), (1, 0)], 4: [(3, 3), (1, 3)], 16: [(0, 3)], 12: [(3, 1), (3, 0)], 10: [(3, 2)], 8: [(1, 2)], 19: [(0, 1), (2, 1)], 18: [(2, 3), (0, 2), (2, 2)], 17: [(0, 0)], 14: [(2, 0)]}
+TKE = {(1, 1): 'V', (2, 2): 'V', (2, 0): 'V', (0, 0): 'V', (3, 3): 'V', (0, 1): 'V', (1, 2): 'S', (2, 3): 'S', (3, 1): 'H', (1, 0): 'H', (0, 3): 'H', (0, 2): 'V', (3, 2): 'V', (1, 3): 'H', (3, 0): 'V', (2, 1): 'V'}
+TE = {12: 'SS', 8: 'SS', 4: 'SS', 0: 'SS', 3: 'SS', 2: 'SS', 13: 'SS', 14: 'SS', 10: 'SS', 1: 'SS', 6: 'SS', 9: 'SS', 7: 'SS', 11: 'SS', 15: 'SS', 5: 'SS'}
+QV = {7: 3, 16: 0, 12: 2, 0: 1}
+RR = {9: [(1, 2), (1, 3)], 7: [(1, 1)], 12: [(0, 2)], 10: [(0, 0)], 14: [(0, 3)], 8: [(1, 0)], 11: [(0, 1)]}
+RRE = {(0, 1): 'V', (0, 3): 'V', (1, 2): 'V', (0, 0): 'V', (1, 3): 'H', (0, 2): 'S', (1, 1): 'H', (1, 0): 'V'}
+OUT = {11: [(0, 1)], 21: [(0, 2), (1, (0, 0)), (1, (0, 3)), (1, (0, 2)), (1, (0, 1))], 17: [(0, 0)], 12: [(0, 3)], 15: [(1, (1, 0))], 9: [(1, (1, 3))], 14: [(1, (1, 1))], 13: [(1, (1, 2))]}
+OUTE = {(1, (0, 3)): 'SSSS', (0, 3): 'SSSS', (1, (1, 3)): 'SSSS', (1, (0, 1)): 'SSSS', (0, 1): 'SSSV', (0, 0): 'SSSV', (1, (0, 2)): 'SSSS', (1, (1, 0)): 'SSSS', (0, 2): 'SSSS', (1, (1, 1)): 'SSSS', (1, (1, 2)): 'SSSS', (1, (0, 0)): 'SSSS'}
+PIECES = {(1, (0, 3)): 4}
 SLOTS = 22
-VSHARE = 20
 
 
 def tile_relativepositionsdpa_pa_v_kernel(tc, queries, v_bias, table, grad_out, dq_out, dr_out):
@@ -43,12 +46,12 @@ def tile_relativepositionsdpa_pa_v_kernel(tc, queries, v_bias, table, grad_out, 
     with ExitStack() as ctx:
         pool = lambda name, bufs: ctx.enter_context(tc.tile_pool(name=name, bufs=bufs))
         const = pool("const", 1)
-        gpool = pool("gpool", 6)
+        gpool = pool("gpool", 3)
         qpool = pool("qpool", 3)
         rpool = pool("rpool", 2)
         stt = pool("stt", 3)
         stk = pool("stk", 3)
-        strq = pool("strq", 2)
+        strq = pool("strq", 3)
         trc = pool("trc", 9)
         tokc = pool("tokc", 6)
         rcp = pool("rcp", 8)
@@ -57,7 +60,7 @@ def tile_relativepositionsdpa_pa_v_kernel(tc, queries, v_bias, table, grad_out, 
         ptr = ctx.enter_context(tc.psum_pool(name="ptr", bufs=4))
         pmm = ctx.enter_context(tc.psum_pool(name="pmm", bufs=4))
 
-        zeros = const.tile([P, K], F32)
+        zeros = const.tile([P, 4, K], F32)
         nc.vector.memset(zeros[:], 0.0)
         ident = const.tile([P, P], F32)
         make_identity(nc, ident[:])
@@ -66,7 +69,7 @@ def tile_relativepositionsdpa_pa_v_kernel(tc, queries, v_bias, table, grad_out, 
         ones = const.tile([P, P], BF16)
         nc.vector.memset(ones[:], 1.0)
         warm = const.tile([P, 1], F32)
-        nc.scalar.mul(warm[:], zeros[:, 0:1], SCALE)
+        nc.scalar.mul(warm[:], zeros[:, 0, 0:1], SCALE)
         vb = const.tile([P, HEADS * K], BF16)
         first = const.tile([1, 16], BF16)
 
@@ -77,26 +80,24 @@ def tile_relativepositionsdpa_pa_v_kernel(tc, queries, v_bias, table, grad_out, 
         def window(base, rows, part):
             return flat[base : base + rows * 4 * ROW].rearrange("(p j c) -> p j c", j=4, c=ROW)
 
-        def load_grad(b, half, parts):
-            if (b, half) not in grad:
-                g = gpool.tile([P, 4, 1024], BF16)
-                grad[b, half] = g
-            g = grad[b, half]
-            if b == 0 and half == 0:
+        def load_grad(b, js):
+            if b not in grad:
+                g = gpool.tile([P, 4, T], BF16)
+                grad[b] = g
+            g = grad[b]
+            if b == 0:
                 nc.sync.dma_start(out=g[:, 1:4, 0:512], in_=window(ROW - S, P, 0)[:, 0:3, 1:513])
                 nc.sync.dma_start(out=g[64:128, 0, 0:512], in_=window(64 * 4 * ROW - S, 64, 0)[:, 0, 1:513])
                 nc.sync.dma_start(out=g[1:65, 0, 0:512], in_=window(4 * ROW - S, 64, 0)[:, 0, 1:513])
-                nc.sync.dma_start(out=g[:, :, 512:1024], in_=window(0, P, 0)[:, :, 1:513])
                 nc.sync.dma_start(out=first[:], in_=flat[0:16].rearrange("(a c) -> a c", a=1))
+                nc.sync.dma_start(out=g[:, :, 512:T], in_=window(0, P, 0)[:, :, 1 : 1 + T - 512])
                 return
-            base, c0 = (0, half * 1024 - 512) if b == 0 else (b * S * T - S, half * 1024)
-            for lo, hi in parts:
-                nc.sync.dma_start(out=g[:, :, lo:hi], in_=window(base, P, 0)[:, :, 1 + c0 + lo : 1 + c0 + hi])
+            j0, j1 = js[0], js[-1] + 1
+            nc.sync.dma_start(out=g[:, j0:j1, :], in_=window(b * S * T - S, P, 0)[:, j0:j1, 1:ROW])
 
         def load(kind, *a):
             if kind == "G":
-                b, half, part = a
-                load_grad(b, half, [(0, 1024)] if part == 2 else [(part * 512, part * 512 + 512)])
+                load_grad(*a)
             elif kind == "Q":
                 q = qpool.tile([P, 4, K], BF16)
                 nc.sync.dma_start(out=q[:], in_=queries[a[0]].rearrange("(p j) k -> p j k", j=4))
@@ -117,12 +118,12 @@ def tile_relativepositionsdpa_pa_v_kernel(tc, queries, v_bias, table, grad_out, 
             rows = slice(T + half * 512, T + half * 512 + 512)
             nc.sync.dma_start(
                 out=dr_out[h, rows, :].rearrange("(p j) k -> p j k", j=4),
-                in_=zeros[:].unsqueeze(1).to_broadcast([P, 4, K]),
+                in_=zeros[:],
             )
 
         def fix_row0(b):
-            g = grad[b, 0]
-            z = zeros[:].bitcast(BF16)
+            g = grad[b]
+            z = zeros[:, 0, :].bitcast(BF16)
             if b == 0:
                 nc.scalar.copy(g[0:1, 0, 0:512], z[0:1, 0:512])
                 nc.scalar.copy(g[0:1, 0, 511:512], first[:, 0:1])
@@ -149,32 +150,38 @@ def tile_relativepositionsdpa_pa_v_kernel(tc, queries, v_bias, table, grad_out, 
                 interleave(dst, src, vcols, 512, nc.scalar.copy)
 
         def trp(u):
-            b, g = u
-            words = grad[b, g // 2][:].rearrange("p j c -> p (j c)").bitcast(F32)
+            b, jp, gp = u
+            words = grad[b][:].rearrange("p j c -> p (j c)").bitcast(F32)
             pair = []
-            for jj in range(2):
+            for q in range(2):
                 bank = ptr.tile([P, 2, 2, P], F32)
-                for j2 in range(2):
+                for j in range(2):
                     for e in range(2):
-                        w0 = (2 * jj + j2) * 512 + (g % 2) * 256
-                        nc.tensor.transpose(bank[:, j2, e, :], words[:, w0 + e : w0 + 256 : 2], ident[:])
+                        w0 = (2 * jp + j) * (T // 2) + (2 * gp + q) * 256
+                        nc.tensor.transpose(bank[:, j, e, :], words[:, w0 + e : w0 + 256 : 2], ident[:])
                 pair.append(bank)
             banks[u] = pair
 
         def trcopy(u, engs):
-            grouped = stt.tile([P, 4, P, 4], BF16, align_bytes=64)
-            for jj, bank in enumerate(banks.pop(u)):
-                dst = grouped[:, 2 * jj : 2 * jj + 2, :, :].rearrange("p j r t -> p (j r t)").bitcast(F32)
+            grouped = stt.tile([P, 2, 2, P, 4], BF16, align_bytes=64)
+            for q, bank in enumerate(banks.pop(u)):
+                dst = grouped[:, q, :, :, :].rearrange("p j r t -> p (j r t)").bitcast(F32)
                 dst = dst.rearrange("p (j r e) -> p j r e", j=2, e=2)
                 src = bank[:].rearrange("p j e r -> p j r e")
-                (nc.scalar.copy if engs[jj] == "S" else nc.vector.tensor_copy)(dst, src)
-            staged["T", u] = grouped[:].rearrange("p j r t -> p (j r t)")
+                (nc.scalar.copy if engs[q] == "S" else nc.vector.tensor_copy)(dst, src)
+            staged["T", u] = grouped[:].rearrange("p q j r t -> p (q j r t)")
 
         def tki(u, vcols):
             b, g = u
-            grouped = stk.tile([P, 512, 4], BF16, align_bytes=64)
-            both(grouped, grad[b, g // 2][:, :, (g % 2) * 512 : (g % 2) * 512 + 512], vcols)
-            staged["K", u] = grouped[:].rearrange("p w t -> p (w t)")
+            kgrouped = stk.tile([P, 4, P, 4], BF16, align_bytes=64)
+            dst = kgrouped[:].rearrange("p i c t -> p c t i")
+            src = grad[b][:, :, g * 512 : g * 512 + 512].rearrange("p t (c i) -> p c t i", i=4)
+            cut = vcols // 4
+            if cut:
+                nc.vector.tensor_copy(dst[:, :cut, :, :], src[:, :cut, :, :])
+            if cut < P:
+                nc.scalar.copy(dst[:, cut:, :, :], src[:, cut:, :, :])
+            staged["K", u] = kgrouped[:].rearrange("p i c t -> p (i c t)")
 
         def rri(u, vcols):
             h, g = u
@@ -217,7 +224,7 @@ def tile_relativepositionsdpa_pa_v_kernel(tc, queries, v_bias, table, grad_out, 
                     product(("K", (b, g)), ("Q", b), slice(m * P, m * P + P), n == 0, n == SEQS - 1, acc)
                 accs.append(acc)
             res = opool.tile([P, 4, 512], F32)
-            view = dr_out[h, g * 512 : g * 512 + 512, :].rearrange("(m p) k -> p m k", p=P)
+            view = dr_out[h, g * 512 : g * 512 + 512, :].rearrange("(p m) k -> p m k", m=4)
             step = 4 // pieces
             for m in range(4):
                 (nc.scalar.copy if engs[m] == "S" else nc.vector.tensor_copy)(res[:, m, :], accs[m][:])
@@ -230,7 +237,8 @@ def tile_relativepositionsdpa_pa_v_kernel(tc, queries, v_bias, table, grad_out, 
             for j in range(4):
                 acc = pmm.tile([P, 512], F32)
                 for g in range(4):
-                    product(("T", (b, g)), ("R", (h, g)), slice(j * P, j * P + P), g == 0, g == 3, acc)
+                    c0 = (g % 2) * 256 + (j % 2) * P
+                    product(("T", (b, j // 2, g // 2)), ("R", (h, g)), slice(c0, c0 + P), g == 0, g == 3, acc)
                 accs.append(acc)
             res = opool.tile([P, 4, 512], F32)
             for j in range(4):
@@ -254,8 +262,8 @@ def tile_relativepositionsdpa_pa_v_kernel(tc, queries, v_bias, table, grad_out, 
                     load(*item)
                 fresh = []
                 if s < 16:
-                    b, g = UNITS[s]
-                    if g == 0:
+                    b, jp, gp = UNITS[s]
+                    if jp == 0 and gp == 0:
                         fix_row0(b)
                     trp(UNITS[s])
                 if s == 0:
@@ -265,25 +273,26 @@ def tile_relativepositionsdpa_pa_v_kernel(tc, queries, v_bias, table, grad_out, 
                         nc.scalar.copy(vb[:, h * K : (h + 1) * K], acc[:])
                 for kind, u in pend:
                     quant(kind, u)
-                for k in TK.get(s, []):
-                    tki(UNITS[k], VCOLS.get(("K", k), VCOLS[0]))
-                    fresh.append(("K", UNITS[k]))
+                for u in TK.get(s, []):
+                    tki(u, VCOLS[TKE.get(u, "V")])
+                    fresh.append(("K", u))
                 if s < 16:
-                    trcopy(UNITS[s], "SS")
+                    trcopy(UNITS[s], TE.get(s, "SS"))
                 if s in QV:
                     qvi(QV[s])
                     fresh.append(("Q", QV[s]))
                 for u in RR.get(s, []):
-                    rri(u, VCOLS.get(("R", u), VCOLS[0]))
+                    rri(u, VCOLS[RRE.get(u, "S")])
                     fresh.append(("R", u))
                 if s < 16:
                     fresh.append(("T", UNITS[s]))
                 pend = fresh
-                engs = "SSSS" if s < VSHARE else "SVSV"
-                if s in O0:
-                    out0(O0[s], engs)
-                if s in O1:
-                    out1(*O1[s], engs, 4 if s == SLOTS - 1 else 1)
+                for kind, u in OUT.get(s, []):
+                    engs = OUTE.get((kind, u), "SSSS")
+                    if kind == 0:
+                        out0(u, engs)
+                    else:
+                        out1(*u, engs, PIECES.get((kind, u), 1))
                 for z in range(ZEROS.get(s, 0)):
                     store_zeros(zi)
                     zi += 1

from contextlib import ExitStack

import concourse.mybir as mybir
from concourse.masks import make_identity

SEQS, HEADS, S, T, L, K = 2, 2, 512, 2048, 3072, 512
NB = SEQS * HEADS
SCALE = K**-0.5

FLOPS = 2 * 2 * NB * S * T * K
BYTES = 2 * (NB * S * K + HEADS * K + HEADS * T * K + NB * S * T) + 4 * (NB * S * K + HEADS * L * K)

F32 = mybir.dt.float32
BF16 = mybir.dt.bfloat16
U32 = mybir.dt.uint32
U8 = mybir.dt.uint8
E4M3 = mybir.dt.float8_e4m3fn_x4
E5M2 = mybir.dt.float8_e5m2_x4
MULT = mybir.AluOpType.mult
ADD = mybir.AluOpType.add

P = 128
ROW = T + 1
VCOLS = {'V': 512, 'S': 0, 'H': 256}

UNITS = [(1, 0, 0), (1, 0, 1), (1, 1, 0), (1, 1, 1), (3, 0, 0), (3, 0, 1), (3, 1, 0), (3, 1, 1), (2, 0, 0), (2, 0, 1), (2, 1, 0), (2, 1, 1), (0, 0, 0), (0, 0, 1), (0, 1, 0), (0, 1, 1)]
LOADS0 = [('G', 1, (0,)), ('V',), ('Q', 1), ('G', 1, (1,)), ('G', 1, (2, 3)), ('G', 3, (0, 1)), ('G', 3, (2, 3))]
LATER = {4: [('Q', 2), ('G', 0, (0,)), ('R', 0, 1), ('Q', 0)], 3: [('R', 0, 0), ('G', 2, (2, 3))], 1: [('G', 2, (0, 1)), ('R', 1, 1)], 0: [('Q', 3), ('R', 1, 0)]}
ZEROS = {8: 1, 9: 1, 7: 1, 13: 1}
TK = {2: [(1, 1), (1, 0)], 4: [(3, 3), (1, 3)], 16: [(0, 3)], 12: [(3, 1), (3, 0)], 10: [(3, 2)], 8: [(1, 2)], 19: [(0, 1), (2, 1)], 18: [(2, 3), (0, 2), (2, 2)], 17: [(0, 0)], 14: [(2, 0)]}
TKE = {(1, 1): 'V', (2, 2): 'V', (2, 0): 'V', (0, 0): 'V', (3, 3): 'V', (0, 1): 'V', (1, 2): 'S', (2, 3): 'S', (3, 1): 'H', (1, 0): 'H', (0, 3): 'H', (0, 2): 'V', (3, 2): 'V', (1, 3): 'H', (3, 0): 'V', (2, 1): 'V'}
TE = {12: 'SS', 8: 'SS', 4: 'SS', 0: 'SS', 3: 'SS', 2: 'SS', 13: 'SS', 14: 'SS', 10: 'SS', 1: 'SS', 6: 'SS', 9: 'SS', 7: 'SS', 11: 'SS', 15: 'SS', 5: 'SS'}
QV = {7: 3, 16: 0, 12: 2, 0: 1}
RR = {9: [(1, 2), (1, 3)], 7: [(1, 1)], 12: [(0, 2)], 10: [(0, 0)], 14: [(0, 3)], 8: [(1, 0)], 11: [(0, 1)]}
RRE = {(0, 1): 'V', (0, 3): 'V', (1, 2): 'V', (0, 0): 'V', (1, 3): 'H', (0, 2): 'S', (1, 1): 'H', (1, 0): 'V'}
OUT = {11: [(0, 1)], 21: [(0, 2), (1, (0, 0)), (1, (0, 3)), (1, (0, 2)), (1, (0, 1))], 17: [(0, 0)], 12: [(0, 3)], 15: [(1, (1, 0))], 9: [(1, (1, 3))], 14: [(1, (1, 1))], 13: [(1, (1, 2))]}
OUTE = {(1, (0, 3)): 'SSSS', (0, 3): 'SSSS', (1, (1, 3)): 'SSSS', (1, (0, 1)): 'SSSS', (0, 1): 'SSSV', (0, 0): 'SSSV', (1, (0, 2)): 'SSSS', (1, (1, 0)): 'SSSS', (0, 2): 'SSSS', (1, (1, 1)): 'SSSS', (1, (1, 2)): 'SSSS', (1, (0, 0)): 'SSSS'}
PIECES = {(1, (0, 3)): 4}
SLOTS = 22


def tile_relativepositionsdpa_pa_v_kernel(tc, queries, v_bias, table, grad_out, dq_out, dr_out):
    nc = tc.nc
    flat = grad_out.rearrange("b s t -> (b s t)")

    with ExitStack() as ctx:
        pool = lambda name, bufs: ctx.enter_context(tc.tile_pool(name=name, bufs=bufs))
        const = pool("const", 1)
        gpool = pool("gpool", 3)
        qpool = pool("qpool", 3)
        rpool = pool("rpool", 2)
        stt = pool("stt", 3)
        stk = pool("stk", 3)
        strq = pool("strq", 3)
        trc = pool("trc", 9)
        tokc = pool("tokc", 6)
        rcp = pool("rcp", 8)
        qcp = pool("qcp", 4)
        opool = pool("opool", 4)
        ptr = ctx.enter_context(tc.psum_pool(name="ptr", bufs=4))
        pmm = ctx.enter_context(tc.psum_pool(name="pmm", bufs=4))

        zeros = const.tile([P, 4, K], F32)
        nc.vector.memset(zeros[:], 0.0)
        ident = const.tile([P, P], F32)
        make_identity(nc, ident[:])
        vrow = const.tile([P, HEADS * K], BF16)
        nc.vector.memset(vrow[:], 0.0)
        ones = const.tile([P, P], BF16)
        nc.vector.memset(ones[:], 1.0)
        warm = const.tile([P, 1], F32)
        nc.scalar.mul(warm[:], zeros[:, 0, 0:1], SCALE)
        vb = const.tile([P, HEADS * K], BF16)
        first = const.tile([1, 16], BF16)

        grad, qraw, rraw = {}, {}, {}
        banks, staged = {}, {}
        codes = {}

        def window(base, rows, part):
            return flat[base : base + rows * 4 * ROW].rearrange("(p j c) -> p j c", j=4, c=ROW)

        def load_grad(b, js):
            if b not in grad:
                g = gpool.tile([P, 4, T], BF16)
                grad[b] = g
            g = grad[b]
            if b == 0:
                nc.sync.dma_start(out=g[:, 1:4, 0:512], in_=window(ROW - S, P, 0)[:, 0:3, 1:513])
                nc.sync.dma_start(out=g[64:128, 0, 0:512], in_=window(64 * 4 * ROW - S, 64, 0)[:, 0, 1:513])
                nc.sync.dma_start(out=g[1:65, 0, 0:512], in_=window(4 * ROW - S, 64, 0)[:, 0, 1:513])
                nc.sync.dma_start(out=first[:], in_=flat[0:16].rearrange("(a c) -> a c", a=1))
                nc.sync.dma_start(out=g[:, :, 512:T], in_=window(0, P, 0)[:, :, 1 : 1 + T - 512])
                return
            j0, j1 = js[0], js[-1] + 1
            nc.sync.dma_start(out=g[:, j0:j1, :], in_=window(b * S * T - S, P, 0)[:, j0:j1, 1:ROW])

        def load(kind, *a):
            if kind == "G":
                load_grad(*a)
            elif kind == "Q":
                q = qpool.tile([P, 4, K], BF16)
                nc.sync.dma_start(out=q[:], in_=queries[a[0]].rearrange("(p j) k -> p j k", j=4))
                qraw[a[0]] = q
            elif kind == "R":
                h, half = a
                r = rpool.tile([P, 2, 4, K], BF16)
                nc.sync.dma_start(
                    out=r[:],
                    in_=table[h, half * 1024 : half * 1024 + 1024, :].rearrange("(g p j) k -> p g j k", p=P, j=4),
                )
                rraw[h, half] = r
            elif kind == "V":
                nc.sync.dma_start(out=vrow[0:1, :], in_=v_bias.rearrange("a h b k -> (a b) (h k)"))

        def store_zeros(i):
            h, half = divmod(i, 2)
            rows = slice(T + half * 512, T + half * 512 + 512)
            nc.sync.dma_start(
                out=dr_out[h, rows, :].rearrange("(p j) k -> p j k", j=4),
                in_=zeros[:],
            )

        def fix_row0(b):
            g = grad[b]
            z = zeros[:, 0, :].bitcast(BF16)
            if b == 0:
                nc.scalar.copy(g[0:1, 0, 0:512], z[0:1, 0:512])
                nc.scalar.copy(g[0:1, 0, 511:512], first[:, 0:1])
            else:
                nc.scalar.copy(g[0:1, 0, 0:511], z[0:1, 0:511])

        def quantize(key, cpool, fmt):
            src = staged.pop(key)
            code = cpool.tile([P, 512], U32, align_bytes=64)
            scale = cpool.tile([P, 512], U8, align_bytes=64)
            nc.vector.quantize_mx(out=code[:].bitcast(fmt), scales=scale[:], in_=src)
            codes[key] = (code, scale)

        def interleave(dst, src, lo, hi, copy):
            copy(
                dst[:, lo:hi, :].rearrange("p (c i) t -> p c t i", i=4),
                src[:, :, lo:hi].rearrange("p t (c i) -> p c t i", i=4),
            )

        def both(dst, src, vcols):
            if vcols:
                interleave(dst, src, 0, vcols, nc.vector.tensor_copy)
            if vcols < 512:
                interleave(dst, src, vcols, 512, nc.scalar.copy)

        def trp(u):
            b, jp, gp = u
            words = grad[b][:].rearrange("p j c -> p (j c)").bitcast(F32)
            pair = []
            for q in range(2):
                bank = ptr.tile([P, 2, 2, P], F32)
                for j in range(2):
                    for e in range(2):
                        w0 = (2 * jp + j) * (T // 2) + (2 * gp + q) * 256
                        nc.tensor.transpose(bank[:, j, e, :], words[:, w0 + e : w0 + 256 : 2], ident[:])
                pair.append(bank)
            banks[u] = pair

        def trcopy(u, engs):
            grouped = stt.tile([P, 2, 2, P, 4], BF16, align_bytes=64)
            for q, bank in enumerate(banks.pop(u)):
                dst = grouped[:, q, :, :, :].rearrange("p j r t -> p (j r t)").bitcast(F32)
                dst = dst.rearrange("p (j r e) -> p j r e", j=2, e=2)
                src = bank[:].rearrange("p j e r -> p j r e")
                (nc.scalar.copy if engs[q] == "S" else nc.vector.tensor_copy)(dst, src)
            staged["T", u] = grouped[:].rearrange("p q j r t -> p (q j r t)")

        def tki(u, vcols):
            b, g = u
            kgrouped = stk.tile([P, 4, P, 4], BF16, align_bytes=64)
            dst = kgrouped[:].rearrange("p i c t -> p c t i")
            src = grad[b][:, :, g * 512 : g * 512 + 512].rearrange("p t (c i) -> p c t i", i=4)
            cut = vcols // 4
            if cut:
                nc.vector.tensor_copy(dst[:, :cut, :, :], src[:, :cut, :, :])
            if cut < P:
                nc.scalar.copy(dst[:, cut:, :, :], src[:, cut:, :, :])
            staged["K", u] = kgrouped[:].rearrange("p i c t -> p (i c t)")

        def rri(u, vcols):
            h, g = u
            rgrouped = strq.tile([P, 512, 4], BF16, align_bytes=64, tag="rq")
            both(rgrouped, rraw[h, g // 2][:, g % 2, :, :], vcols)
            staged["R", u] = rgrouped[:].rearrange("p w t -> p (w t)")

        def qvi(b):
            h = b % HEADS
            qgrouped = strq.tile([P, 512, 4], BF16, align_bytes=64, tag="rq")
            bias = vb[:, h * K : (h + 1) * K].unsqueeze(2).to_broadcast([P, K, 4])
            nc.vector.scalar_tensor_tensor(
                out=qgrouped[:],
                in0=qraw[b][:].rearrange("p t w -> p w t"),
                scalar=SCALE,
                in1=bias,
                op0=MULT,
                op1=ADD,
            )
            staged["Q", b] = qgrouped[:].rearrange("p w t -> p (w t)")

        def product(lhs, rhs, cols, start, stop, acc):
            (lc, ls), (rc, rs) = codes[lhs], codes[rhs]
            nc.tensor.matmul_mx(
                out=acc[:],
                lhsT=lc[:, cols].bitcast(E5M2),
                lhsT_scale=ls[:, cols],
                rhs=rc[:].bitcast(E4M3),
                rhs_scale=rs[:],
                start=start,
                stop=stop,
            )

        def out1(h, g, engs, pieces):
            accs = []
            for m in range(4):
                acc = pmm.tile([P, 512], F32)
                for n in range(SEQS):
                    b = n * HEADS + h
                    product(("K", (b, g)), ("Q", b), slice(m * P, m * P + P), n == 0, n == SEQS - 1, acc)
                accs.append(acc)
            res = opool.tile([P, 4, 512], F32)
            view = dr_out[h, g * 512 : g * 512 + 512, :].rearrange("(p m) k -> p m k", m=4)
            step = 4 // pieces
            for m in range(4):
                (nc.scalar.copy if engs[m] == "S" else nc.vector.tensor_copy)(res[:, m, :], accs[m][:])
                if (m + 1) % step == 0:
                    nc.sync.dma_start(out=view[:, m + 1 - step : m + 1, :], in_=res[:, m + 1 - step : m + 1, :])

        def out0(b, engs):
            h = b % HEADS
            accs = []
            for j in range(4):
                acc = pmm.tile([P, 512], F32)
                for g in range(4):
                    c0 = (g % 2) * 256 + (j % 2) * P
                    product(("T", (b, j // 2, g // 2)), ("R", (h, g)), slice(c0, c0 + P), g == 0, g == 3, acc)
                accs.append(acc)
            res = opool.tile([P, 4, 512], F32)
            for j in range(4):
                if engs[j] == "S":
                    nc.scalar.mul(res[:, j, :], accs[j][:], SCALE)
                else:
                    nc.vector.tensor_scalar(res[:, j, :], accs[j][:], SCALE, None, op0=MULT)
            nc.sync.dma_start(out=dq_out[b].rearrange("(p j) k -> p j k", j=4), in_=res[:])

        def quant(kind, u):
            cpool = {"T": trc, "K": tokc, "R": rcp, "Q": qcp}[kind]
            quantize((kind, u), cpool, E5M2 if kind in "TK" else E4M3)

        with tc.manual_schedule():
            for item in LOADS0:
                load(*item)
            pend = []
            zi = 0
            for s in range(SLOTS):
                for item in LATER.get(s, []):
                    load(*item)
                fresh = []
                if s < 16:
                    b, jp, gp = UNITS[s]
                    if jp == 0 and gp == 0:
                        fix_row0(b)
                    trp(UNITS[s])
                if s == 0:
                    for h in range(HEADS):
                        acc = pmm.tile([P, 512], F32)
                        nc.tensor.matmul(acc[:], lhsT=ones[:], rhs=vrow[:, h * K : (h + 1) * K], start=True, stop=True)
                        nc.scalar.copy(vb[:, h * K : (h + 1) * K], acc[:])
                for kind, u in pend:
                    quant(kind, u)
                for u in TK.get(s, []):
                    tki(u, VCOLS[TKE.get(u, "V")])
                    fresh.append(("K", u))
                if s < 16:
                    trcopy(UNITS[s], TE.get(s, "SS"))
                if s in QV:
                    qvi(QV[s])
                    fresh.append(("Q", QV[s]))
                for u in RR.get(s, []):
                    rri(u, VCOLS[RRE.get(u, "S")])
                    fresh.append(("R", u))
                if s < 16:
                    fresh.append(("T", UNITS[s]))
                pend = fresh
                for kind, u in OUT.get(s, []):
                    engs = OUTE.get((kind, u), "SSSS")
                    if kind == 0:
                        out0(u, engs)
                    else:
                        out1(*u, engs, PIECES.get((kind, u), 1))
                for z in range(ZEROS.get(s, 0)):
                    store_zeros(zi)
                    zi += 1
